import numpy as np
import ml_dtypes


def mxq(x, axis, fmt="e4m3"):
    dtype, down = {"e4m3": (ml_dtypes.float8_e4m3fn, 7), "e5m2": (ml_dtypes.float8_e5m2, 14)}[fmt]
    v = np.moveaxis(np.asarray(x, np.float32).astype(ml_dtypes.bfloat16).astype(np.float64), axis, -1)
    blocks = v.reshape(v.shape[:-1] + (-1, 32))
    amax = np.abs(blocks).max(-1, keepdims=True)
    byte = np.maximum(np.where(amax > 0, np.frexp(amax)[1] - 1 + 127, 0) - down, 1)
    scale = np.exp2(byte - 127.0)
    codes = (blocks / scale).astype(np.float32).astype(dtype).astype(np.float64)
    return np.moveaxis((codes * scale).reshape(v.shape), -1, axis)


WIDE = False


def mx_kscale(k):
    if not WIDE:
        return np.ones(k)
    levels = np.array([10, -10, 5, -5, 0])
    a = np.random.permutation(np.resize(levels, k // 512 * 4)).reshape(k // 512, 4)
    idx = np.arange(k)
    return np.exp2(a[idx // 512, idx % 128 // 32])


BF16 = ml_dtypes.bfloat16


def bf(x):
    return np.asarray(x, np.float32).astype(BF16)


def f64(x):
    return np.asarray(x).astype(np.float64)


E2M1 = np.array([0.0, 0.5, 1.0, 1.5, 2.0, 3.0, 4.0, 6.0, -0.0, -0.5, -1.0, -1.5, -2.0, -3.0, -4.0, -6.0])


def pack_weight(w, fmt):
    k, n = w.shape
    w = f64(bf(w)).reshape(k // 32, 32, n)
    amax = np.abs(w).max(1)
    if fmt == "e4m3":
        byte = np.frexp(amax)[1] - 1 + 127 - 7
    else:
        mant, ex = np.frexp(amax / 6.0)
        byte = np.where(mant > 0.5, ex, ex - 1) + 127
    byte = np.clip(np.where(amax > 0, byte, 1), 1, 254)
    scaled = (w * np.exp2(127.0 - byte)[:, None, :]).reshape(k, n).astype(np.float32)
    by_word = np.ascontiguousarray(scaled.reshape(k // 512, 128, 4, n).transpose(0, 1, 3, 2))
    if fmt == "e4m3":
        words = by_word.astype(ml_dtypes.float8_e4m3fn).view(np.uint8)
    else:
        c = by_word.astype(ml_dtypes.float4_e2m1fn).view(np.uint8) & 0xF
        words = c[..., 0::2] | (c[..., 1::2] << 4)
    return np.ascontiguousarray(words), np.ascontiguousarray(byte.astype(np.uint8).reshape(k // 512, 16, n))


def unpack_weight(words, scales, fmt):
    g, p, n, _ = words.shape
    if fmt == "e4m3":
        vals = np.ascontiguousarray(words).view(ml_dtypes.float8_e4m3fn).astype(np.float64)
    else:
        nib = np.empty((g, p, n, 4), np.uint8)
        nib[..., 0::2] = words & 0xF
        nib[..., 1::2] = words >> 4
        vals = E2M1[nib]
    vals = vals * np.repeat(np.exp2(scales.astype(np.float64) - 127.0), 8, axis=1)[..., None]
    return vals.transpose(0, 1, 3, 2).reshape(g * 512, n)


N, T, D, B0, C, P0, V1, P1, V2 = 2, 64, 16384, 1022, 2, 512, 1024, 512, 1024
MU = 0.25
SIG = 2.0
FMT = "e4m3"


def softmax(v):
    e = np.exp(v - v.max(-1, keepdims=True))
    return e / e.sum(-1, keepdims=True)


def setup_inputs():
    s, t = mx_kscale(D), mx_kscale(P0)
    hw = np.random.standard_normal((D, B0 + C)) * SIG / np.sqrt(D)
    hw[:, B0:] = hw[:, B0:] / SIG + (np.log(B0) + 0.5 * SIG * SIG) / (MU * D)
    x = bf((np.random.standard_normal((N, T, D)) + MU) * s)
    head_words, head_scales = pack_weight(hw / s[:, None], FMT)
    proj_words, proj_scales = pack_weight(np.random.standard_normal((D, P0)) / np.sqrt(D) / s[:, None] * t, FMT)
    tail_words, tail_scales = pack_weight(np.random.standard_normal((P0, V1)) * SIG / np.sqrt(P0) / t[:, None], FMT)
    return {"x": x,
            "head_weight_words": head_words, "head_weight_scales": head_scales,
            "tail_proj_0_words": proj_words, "tail_proj_0_scales": proj_scales,
            "tail_w_0_words": tail_words, "tail_w_0_scales": tail_scales}


def reference(x, head_weight_words, head_weight_scales, tail_proj_0_words, tail_proj_0_scales, tail_w_0_words, tail_w_0_scales):
    xq = mxq(f64(x), 2, "e4m3")
    head_sm = softmax(xq @ unpack_weight(head_weight_words, head_weight_scales, FMT))
    h = xq @ unpack_weight(tail_proj_0_words, tail_proj_0_scales, FMT)
    tail_sm = softmax(mxq(h, 2, "e4m3") @ unpack_weight(tail_w_0_words, tail_w_0_scales, FMT))
    probs = np.concatenate([head_sm[..., :B0], tail_sm * head_sm[..., B0:B0 + 1]], axis=-1)
    return probs, head_sm[..., B0 + 1:B0 + C]

@@ -1,0 +1,290 @@
+from contextlib import ExitStack
+
+import concourse.mybir as mybir
+from concourse.masks import make_identity
+
+F32 = mybir.dt.float32
+BF16 = mybir.dt.bfloat16
+I32 = mybir.dt.int32
+U32 = mybir.dt.uint32
+U8 = mybir.dt.uint8
+FP8X4 = mybir.dt.float8_e4m3fn_x4
+EXP = mybir.ActivationFunctionType.Exp
+COPY = mybir.ActivationFunctionType.Copy
+MULT = mybir.AluOpType.mult
+MAX = mybir.AluOpType.max
+X_AXIS = mybir.AxisListType.X
+
+P = 128
+PACK = 4
+K_PASS = P * PACK
+D = 16384
+GROUPS = D // K_PASS
+BANK = 512
+HEAD_N = 1024
+HEAD_TOKENS = 1022
+PROJ_N = 512
+TAIL_N = 1024
+HALVES = 2
+SCALE_ROWS = K_PASS // 32
+PLANE_OFFSETS = 4
+PLANE_SLOTS = GROUPS // PLANE_OFFSETS
+
+X_CHUNK_GROUPS = 8
+QUANT_GROUPS = 4
+BANK_GROUPS = 2
+PROJ_TILE_GROUPS = 4
+HEAD_TILE_GROUPS = 2
+
+FLOPS = 2 * P * D * (HEAD_N + PROJ_N) + 2 * P * PROJ_N * TAIL_N
+
+
+def words_by_partition(words):
+    return words.rearrange("g p n t -> p g (n t)").bitcast(I32)
+
+
+def load_scale_planes(nc, planes, scales):
+    slots = planes.shape[1]
+    for q in range(SCALE_ROWS):
+        first = 32 * (q // 4) + q % 4
+        nc.sync.dma_start(
+            out=planes[first : first + 4 * PLANE_OFFSETS : 4].bitcast(I32),
+            in_=scales[:, q, :].rearrange("(j a) n -> j a n", a=slots).bitcast(I32),
+        )
+
+
+def plane_of_group(planes, g, columns):
+    slots = planes.shape[1]
+    return planes[4 * (g // slots) : P, g % slots, columns]
+
+
+def exp_and_reciprocal(nc, small, logits, exps, label):
+    bank_max = small.tile([P, HALVES], F32, name=label + "_bank_max")
+    for b in range(HALVES):
+        nc.vector.reduce_max(out=bank_max[:, b : b + 1], in_=logits[b][:], axis=X_AXIS)
+    neg_max = small.tile([P, 1], F32, name=label + "_neg_max")
+    nc.vector.tensor_scalar(
+        out=neg_max[:],
+        in0=bank_max[:, 0:1],
+        scalar1=bank_max[:, 1:2],
+        scalar2=-1.0,
+        op0=MAX,
+        op1=MULT,
+    )
+    bank_sum = small.tile([P, HALVES], F32, name=label + "_bank_sum")
+    for b in range(HALVES):
+        nc.scalar.activation(
+            out=exps[:, b * BANK : (b + 1) * BANK],
+            in_=logits[b][:],
+            func=EXP,
+            bias=neg_max[:],
+            scale=1.0,
+            accum_out=bank_sum[:, b : b + 1],
+        )
+    total = small.tile([P, 1], F32, name=label + "_total")
+    nc.vector.tensor_add(out=total[:], in0=bank_sum[:, 0:1], in1=bank_sum[:, 1:2])
+    recip = small.tile([P, 1], F32, name=label + "_recip")
+    nc.vector.reciprocal(out=recip[:], in_=total[:])
+    return recip
+
+
+def tile_adaptiveinputsoftmax_pa_k_kernel(
+    tc,
+    x,
+    head_weight_words,
+    head_weight_scales,
+    tail_proj_0_words,
+    tail_proj_0_scales,
+    tail_w_0_words,
+    tail_w_0_scales,
+    out_0,
+    out_1,
+):
+    nc = tc.nc
+    x_rows = x.flatten_outer_dims()
+    probs_rows = out_0.flatten_outer_dims()
+    other_row = out_1.rearrange("a b c -> c (a b)")
+    head_words = words_by_partition(head_weight_words)
+    proj_words = words_by_partition(tail_proj_0_words)
+    tail_words = words_by_partition(tail_w_0_words)
+
+    with ExitStack() as stack:
+        keep = stack.enter_context(tc.tile_pool(name="keep", bufs=1))
+        small = stack.enter_context(tc.tile_pool(name="small", bufs=1))
+        x_pool = stack.enter_context(tc.tile_pool(name="x_pool", bufs=4))
+        stage = stack.enter_context(tc.tile_pool(name="stage", bufs=3))
+        proj_pool = stack.enter_context(tc.tile_pool(name="proj_pool", bufs=8))
+        head_pool = stack.enter_context(tc.tile_pool(name="head_pool", bufs=6))
+        psum = stack.enter_context(tc.psum_pool(name="psum", bufs=1))
+
+        ident_f32 = keep.tile([P, P], F32)
+        make_identity(nc, ident_f32[:])
+        ident_bf16 = keep.tile([P, P], BF16)
+        make_identity(nc, ident_bf16[:])
+
+        proj_planes = keep.tile([P, PLANE_SLOTS, PROJ_N], U8, align_bytes=64)
+        tail_planes = keep.tile([P, 1, TAIL_N], U8, align_bytes=64)
+        head_planes = keep.tile([P, PLANE_SLOTS, HEAD_N], U8, align_bytes=64)
+        for planes in (proj_planes, tail_planes, head_planes):
+            nc.vector.memset(planes[:].bitcast(I32), 0)
+
+        chunk_columns = X_CHUNK_GROUPS * K_PASS
+        x_chunks = []
+        for c in range(GROUPS // X_CHUNK_GROUPS):
+            x_chunk = x_pool.tile([P, chunk_columns], BF16)
+            nc.sync.dma_start(
+                out=x_chunk[:], in_=x_rows[:, c * chunk_columns : (c + 1) * chunk_columns]
+            )
+            x_chunks.append(x_chunk)
+        load_scale_planes(nc, proj_planes, tail_proj_0_scales)
+
+        x_codes = keep.tile([P, GROUPS * P], U32, align_bytes=64)
+        x_scales = keep.tile([P, GROUPS * P], U8, align_bytes=64)
+        for c in range(GROUPS // X_CHUNK_GROUPS):
+            x_chunk = x_chunks[c]
+            x_pairs = x_chunk[:].bitcast(F32)
+            for call in range(X_CHUNK_GROUPS // QUANT_GROUPS):
+                grouped = stage.tile([P, QUANT_GROUPS * K_PASS], BF16, align_bytes=64)
+                grouped_pairs = grouped[:].bitcast(F32)
+                for bank in range(QUANT_GROUPS // BANK_GROUPS):
+                    xt = psum.tile([P, BANK_GROUPS, 2, P], F32, tag="transposed", bufs=3)
+                    for gi in range(BANK_GROUPS):
+                        first = (K_PASS // 2) * (call * QUANT_GROUPS + bank * BANK_GROUPS + gi)
+                        for u in range(2):
+                            nc.tensor.transpose(
+                                xt[:, gi, u, :],
+                                x_pairs[:, first + u : first + K_PASS // 2 : 2],
+                                ident_f32[:],
+                            )
+                    pairs_out = grouped_pairs[:, bank * BANK : (bank + 1) * BANK].rearrange(
+                        "p (g r u) -> p g r u", g=BANK_GROUPS, u=2
+                    )
+                    pairs_in = xt[:].rearrange("p g u r -> p g r u")
+                    if bank % 2 == 0:
+                        nc.scalar.copy(out=pairs_out, in_=pairs_in)
+                    else:
+                        nc.vector.tensor_copy(out=pairs_out, in_=pairs_in)
+                g0 = c * X_CHUNK_GROUPS + call * QUANT_GROUPS
+                columns = slice(g0 * P, (g0 + QUANT_GROUPS) * P)
+                nc.vector.quantize_mx(
+                    out=x_codes[:, columns].bitcast(FP8X4),
+                    scales=x_scales[:, columns],
+                    in_=grouped[:],
+                )
+
+        def x_pass(acc, g, weight_words, weight_plane):
+            nc.tensor.matmul_mx(
+                out=acc[:],
+                lhsT=x_codes[:, g * P : (g + 1) * P].bitcast(FP8X4),
+                lhsT_scale=x_scales[:, g * P : (g + 1) * P],
+                rhs=weight_words.bitcast(FP8X4),
+                rhs_scale=weight_plane,
+                start=(g == 0),
+                stop=(g == GROUPS - 1),
+            )
+
+        h_acc = psum.tile([P, PROJ_N], F32)
+        for i in range(GROUPS // PROJ_TILE_GROUPS):
+            proj_tile = proj_pool.tile([P, PROJ_TILE_GROUPS, PROJ_N], U32, align_bytes=64)
+            nc.sync.dma_start(
+                out=proj_tile[:].bitcast(I32),
+                in_=proj_words[:, i * PROJ_TILE_GROUPS : (i + 1) * PROJ_TILE_GROUPS, :],
+            )
+            for gi in range(PROJ_TILE_GROUPS):
+                g = i * PROJ_TILE_GROUPS + gi
+                x_pass(
+                    h_acc, g, proj_tile[:, gi, :], plane_of_group(proj_planes, g, slice(0, PROJ_N))
+                )
+
+        tail_tile = keep.tile([P, TAIL_N], U32, align_bytes=64)
+        nc.sync.dma_start(out=tail_tile[:].bitcast(I32), in_=tail_words[:, 0, :])
+        for r in range(4):
+            nc.sync.dma_start(
+                out=tail_planes[r:P:32, 0, :].bitcast(I32),
+                in_=tail_w_0_scales[0, r:SCALE_ROWS:4, :].bitcast(I32),
+            )
+        load_scale_planes(nc, head_planes, head_weight_scales)
+
+        h_sorted = small.tile([P, PACK, P], BF16)
+        nc.scalar.copy(out=h_sorted[:], in_=h_acc[:].rearrange("r (p t) -> r t p", t=PACK))
+        ht = psum.tile([P, PACK, P], BF16, tag="transposed", bufs=3)
+        for t in range(PACK):
+            nc.tensor.transpose(ht[:, t, :], h_sorted[:, t, :], ident_bf16[:])
+        h_grouped = small.tile([P, P, PACK], BF16, align_bytes=64)
+        nc.vector.tensor_copy(out=h_grouped[:], in_=ht[:].rearrange("p t r -> p r t"))
+        h_codes = small.tile([P, P], U32, align_bytes=64)
+        h_scales = small.tile([P, P], U8, align_bytes=64)
+        nc.vector.quantize_mx(
+            out=h_codes[:].bitcast(FP8X4),
+            scales=h_scales[:],
+            in_=h_grouped[:].rearrange("p r t -> p (r t)"),
+        )
+        tail_logits = []
+        for b in range(HALVES):
+            columns = slice(b * BANK, (b + 1) * BANK)
+            logits = psum.tile([P, BANK], F32, name="tail_logits%d" % b)
+            nc.tensor.matmul_mx(
+                out=logits[:],
+                lhsT=h_codes[:].bitcast(FP8X4),
+                lhsT_scale=h_scales[:],
+                rhs=tail_tile[:, columns].bitcast(FP8X4),
+                rhs_scale=plane_of_group(tail_planes, 0, columns),
+                start=True,
+                stop=True,
+            )
+            tail_logits.append(logits)
+        tail_exp = keep.tile([P, TAIL_N], F32)
+        tail_recip = exp_and_reciprocal(nc, small, tail_logits, tail_exp, "tail")
+
+        head_logits = []
+        for b in range(HALVES):
+            logits = psum.tile([P, BANK], F32, name="head_logits%d" % b)
+            head_logits.append(logits)
+        for i in range(GROUPS // HEAD_TILE_GROUPS):
+            head_tile = head_pool.tile([P, HEAD_TILE_GROUPS, HEAD_N], U32, align_bytes=64)
+            nc.sync.dma_start(
+                out=head_tile[:].bitcast(I32),
+                in_=head_words[:, i * HEAD_TILE_GROUPS : (i + 1) * HEAD_TILE_GROUPS, :],
+            )
+            for b in range(HALVES):
+                columns = slice(b * BANK, (b + 1) * BANK)
+                for gi in range(HEAD_TILE_GROUPS):
+                    g = i * HEAD_TILE_GROUPS + gi
+                    x_pass(
+                        head_logits[b],
+                        g,
+                        head_tile[:, gi, columns],
+                        plane_of_group(head_planes, g, columns),
+                    )
+
+        head_exp = keep.tile([P, HEAD_N], F32)
+        head_recip = exp_and_reciprocal(nc, small, head_logits, head_exp, "head")
+
+        tail_factor = small.tile([P, 1], F32)
+        nc.vector.tensor_scalar(
+            out=tail_factor[:],
+            in0=head_exp[:, HEAD_TOKENS : HEAD_TOKENS + 1],
+            scalar1=head_recip[:],
+            scalar2=tail_recip[:],
+            op0=MULT,
+            op1=MULT,
+        )
+        nc.scalar.activation(out=tail_exp[:], in_=tail_exp[:], func=COPY, scale=tail_factor[:])
+        nc.sync.dma_start(out=probs_rows[:, HEAD_TOKENS : HEAD_TOKENS + TAIL_N], in_=tail_exp[:])
+
+        other = small.tile([P, P], F32)
+        nc.vector.tensor_scalar_mul(
+            out=other[:],
+            in0=head_exp[:, HEAD_N - 1 : HEAD_N].to_broadcast([P, P]),
+            scalar1=head_recip[:],
+        )
+        other_t = psum.tile([P, P], F32, tag="transposed", bufs=3)
+        nc.tensor.transpose(other_t[:], other[:], ident_f32[:])
+        other_rows = small.tile([P, P], F32)
+        nc.vector.tensor_copy(out=other_rows[:], in_=other_t[:])
+
+        nc.vector.tensor_scalar_mul(
+            out=head_exp[:, 0:HEAD_TOKENS], in0=head_exp[:, 0:HEAD_TOKENS], scalar1=head_recip[:]
+        )
+        nc.sync.dma_start(out=probs_rows[:, 0:HEAD_TOKENS], in_=head_exp[:, 0:HEAD_TOKENS])
+        nc.sync.dma_start(out=other_row, in_=other_rows[0:1, :])

@@ -11,6 +11,7 @@ U8 = mybir.dt.uint8
 FP8X4 = mybir.dt.float8_e4m3fn_x4
 EXP = mybir.ActivationFunctionType.Exp
 COPY = mybir.ActivationFunctionType.Copy
+ADD = mybir.AluOpType.add
 MULT = mybir.AluOpType.mult
 MAX = mybir.AluOpType.max
 X_AXIS = mybir.AxisListType.X
@@ -35,6 +36,9 @@ QUANT_GROUPS = 4
 BANK_GROUPS = 2
 PROJ_TILE_GROUPS = 4
 HEAD_TILE_GROUPS = 2
+HEAD_SPLIT_GROUPS = 4
+TAIL_ON_SCALAR = 688
+HEAD_LAST_LOADS = (2, 1, 1)
 
 FLOPS = 2 * P * D * (HEAD_N + PROJ_N) + 2 * P * PROJ_N * TAIL_N
 
@@ -240,51 +244,119 @@ def tile_adaptiveinputsoftmax_pa_k_kernel(
         for b in range(HALVES):
             logits = psum.tile([P, BANK], F32, name="head_logits%d" % b)
             head_logits.append(logits)
-        for i in range(GROUPS // HEAD_TILE_GROUPS):
+        half_columns = [slice(b * BANK, (b + 1) * BANK) for b in range(HALVES)]
+        split_from = GROUPS - HEAD_SPLIT_GROUPS
+        for i in range(split_from // HEAD_TILE_GROUPS):
             head_tile = head_pool.tile([P, HEAD_TILE_GROUPS, HEAD_N], U32, align_bytes=64)
             nc.sync.dma_start(
                 out=head_tile[:].bitcast(I32),
                 in_=head_words[:, i * HEAD_TILE_GROUPS : (i + 1) * HEAD_TILE_GROUPS, :],
             )
             for b in range(HALVES):
-                columns = slice(b * BANK, (b + 1) * BANK)
                 for gi in range(HEAD_TILE_GROUPS):
                     g = i * HEAD_TILE_GROUPS + gi
                     x_pass(
                         head_logits[b],
                         g,
-                        head_tile[:, gi, columns],
-                        plane_of_group(head_planes, g, columns),
+                        head_tile[:, gi, half_columns[b]],
+                        plane_of_group(head_planes, g, half_columns[b]),
                     )
+        for b, loads in enumerate(((HEAD_SPLIT_GROUPS,), HEAD_LAST_LOADS)):
+            half_tile = head_pool.tile([P, HEAD_SPLIT_GROUPS, BANK], U32, align_bytes=64, tag="head_tile")
+            first = 0
+            for count in loads:
+                nc.sync.dma_start(
+                    out=half_tile[:, first : first + count, :].bitcast(I32),
+                    in_=head_words[:, split_from + first : split_from + first + count, half_columns[b]],
+                )
+                first += count
+            for gi in range(HEAD_SPLIT_GROUPS):
+                g = split_from + gi
+                x_pass(
+                    head_logits[b],
+                    g,
+                    half_tile[:, gi, :],
+                    plane_of_group(head_planes, g, half_columns[b]),
+                )
 
         head_exp = keep.tile([P, HEAD_N], F32)
-        head_recip = exp_and_reciprocal(nc, small, head_logits, head_exp, "head")
+        max0 = small.tile([P, 1], F32)
+        nc.vector.reduce_max(out=max0[:], in_=head_logits[0][:], axis=X_AXIS)
+        neg_max0 = small.tile([P, 1], F32)
+        nc.vector.tensor_scalar_mul(out=neg_max0[:], in0=max0[:], scalar1=-1.0)
+        sum0 = small.tile([P, 1], F32)
+        nc.scalar.activation(
+            out=head_exp[:, half_columns[0]],
+            in_=head_logits[0][:],
+            func=EXP,
+            bias=neg_max0[:],
+            scale=1.0,
+            accum_out=sum0[:],
+        )
+        max1 = small.tile([P, 1], F32)
+        nc.vector.reduce_max(out=max1[:], in_=head_logits[1][:], axis=X_AXIS)
+        neg_max = small.tile([P, 1], F32)
+        nc.vector.tensor_scalar(
+            out=neg_max[:], in0=max1[:], scalar1=max0[:], scalar2=-1.0, op0=MAX, op1=MULT
+        )
+        shift0 = small.tile([P, 1], F32)
+        nc.scalar.activation(out=shift0[:], in_=max0[:], func=EXP, bias=neg_max[:], scale=1.0)
+        sum1 = small.tile([P, 1], F32)
+        nc.scalar.activation(
+            out=head_exp[:, half_columns[1]],
+            in_=head_logits[1][:],
+            func=EXP,
+            bias=neg_max[:],
+            scale=1.0,
+            accum_out=sum1[:],
+        )
+        total = small.tile([P, 1], F32)
+        nc.vector.scalar_tensor_tensor(
+            out=total[:], in0=sum0[:], scalar=shift0[:], in1=sum1[:], op0=MULT, op1=ADD
+        )
+        recip = small.tile([P, 1], F32)
+        nc.vector.reciprocal(out=recip[:], in_=total[:])
 
         tail_factor = small.tile([P, 1], F32)
         nc.vector.tensor_scalar(
             out=tail_factor[:],
             in0=head_exp[:, HEAD_TOKENS : HEAD_TOKENS + 1],
-            scalar1=head_recip[:],
+            scalar1=recip[:],
             scalar2=tail_recip[:],
             op0=MULT,
             op1=MULT,
         )
-        nc.scalar.activation(out=tail_exp[:], in_=tail_exp[:], func=COPY, scale=tail_factor[:])
-        nc.sync.dma_start(out=probs_rows[:, HEAD_TOKENS : HEAD_TOKENS + TAIL_N], in_=tail_exp[:])
-
-        other = small.tile([P, P], F32)
-        nc.vector.tensor_scalar_mul(
-            out=other[:],
-            in0=head_exp[:, HEAD_N - 1 : HEAD_N].to_broadcast([P, P]),
-            scalar1=head_recip[:],
+        nc.scalar.activation(
+            out=tail_exp[:, 0:TAIL_ON_SCALAR],
+            in_=tail_exp[:, 0:TAIL_ON_SCALAR],
+            func=COPY,
+            scale=tail_factor[:],
         )
-        other_t = psum.tile([P, P], F32, tag="transposed", bufs=3)
-        nc.tensor.transpose(other_t[:], other[:], ident_f32[:])
-        other_rows = small.tile([P, P], F32)
-        nc.vector.tensor_copy(out=other_rows[:], in_=other_t[:])
-
+        other = small.tile([P, 1], F32)
         nc.vector.tensor_scalar_mul(
-            out=head_exp[:, 0:HEAD_TOKENS], in0=head_exp[:, 0:HEAD_TOKENS], scalar1=head_recip[:]
+            out=other[:], in0=head_exp[:, HEAD_N - 1 : HEAD_N], scalar1=recip[:]
+        )
+        nc.vector.tensor_scalar_mul(
+            out=head_exp[:, BANK:HEAD_TOKENS], in0=head_exp[:, BANK:HEAD_TOKENS], scalar1=recip[:]
+        )
+        nc.vector.tensor_scalar(
+            out=head_exp[:, 0:BANK],
+            in0=head_exp[:, 0:BANK],
+            scalar1=recip[:],
+            scalar2=shift0[:],
+            op0=MULT,
+            op1=MULT,
         )
         nc.sync.dma_start(out=probs_rows[:, 0:HEAD_TOKENS], in_=head_exp[:, 0:HEAD_TOKENS])
-        nc.sync.dma_start(out=other_row, in_=other_rows[0:1, :])
+        nc.vector.tensor_scalar_mul(
+            out=tail_exp[:, TAIL_ON_SCALAR:], in0=tail_exp[:, TAIL_ON_SCALAR:], scalar1=tail_factor[:]
+        )
+        nc.sync.dma_start(out=probs_rows[:, HEAD_TOKENS : HEAD_TOKENS + TAIL_N], in_=tail_exp[:])
+
+        other_t = psum.tile([P, P], F32, tag="transposed", bufs=3)
+        nc.tensor.matmul(
+            other_t[:], lhsT=other[:].to_broadcast([P, P]), rhs=ident_f32[:], start=True, stop=True
+        )
+        other_values = small.tile([1, P], F32)
+        nc.vector.tensor_copy(out=other_values[:], in_=other_t[0:1, :])
+        nc.sync.dma_start(out=other_row, in_=other_values[:])

@@ -36,6 +36,10 @@ QUANT_GROUPS = 4
 BANK_GROUPS = 2
 PROJ_TILE_GROUPS = 4
 HEAD_TILE_GROUPS = 2
+
+UPPER_ROWS = range(8, SCALE_ROWS)
+PROJ_ROWS_AFTER_X = ((), range(0, 4), range(4, 8), UPPER_ROWS)
+HEAD_ROWS_AFTER_PROJ = ((), (0, 1), (2, 3), (4, 5), (6, 7), (), (), ())
 HEAD_SPLIT_GROUPS = 4
 TAIL_ON_SCALAR = 688
 HEAD_LAST_LOADS = (2, 1, 1)
@@ -47,14 +51,13 @@ def words_by_partition(words):
     return words.rearrange("g p n t -> p g (n t)").bitcast(I32)
 
 
-def load_scale_planes(nc, planes, scales):
+def load_scale_row(nc, planes, scales, q):
     slots = planes.shape[1]
-    for q in range(SCALE_ROWS):
-        first = 32 * (q // 4) + q % 4
-        nc.sync.dma_start(
-            out=planes[first : first + 4 * PLANE_OFFSETS : 4].bitcast(I32),
-            in_=scales[:, q, :].rearrange("(j a) n -> j a n", a=slots).bitcast(I32),
-        )
+    first = 32 * (q // 4) + q % 4
+    nc.sync.dma_start(
+        out=planes[first : first + 4 * PLANE_OFFSETS : 4].bitcast(I32),
+        in_=scales[:, q, :].rearrange("(j a) n -> j a n", a=slots).bitcast(I32),
+    )
 
 
 def plane_of_group(planes, g, columns):
@@ -140,7 +143,8 @@ def tile_adaptiveinputsoftmax_pa_k_kernel(
                 out=x_chunk[:], in_=x_rows[:, c * chunk_columns : (c + 1) * chunk_columns]
             )
             x_chunks.append(x_chunk)
-        load_scale_planes(nc, proj_planes, tail_proj_0_scales)
+            for q in PROJ_ROWS_AFTER_X[c]:
+                load_scale_row(nc, proj_planes, tail_proj_0_scales, q)
 
         x_codes = keep.tile([P, GROUPS * P], U32, align_bytes=64)
         x_scales = keep.tile([P, GROUPS * P], U8, align_bytes=64)
@@ -194,20 +198,23 @@ def tile_adaptiveinputsoftmax_pa_k_kernel(
                 out=proj_tile[:].bitcast(I32),
                 in_=proj_words[:, i * PROJ_TILE_GROUPS : (i + 1) * PROJ_TILE_GROUPS, :],
             )
+            for q in HEAD_ROWS_AFTER_PROJ[i]:
+                load_scale_row(nc, head_planes, head_weight_scales, q)
             for gi in range(PROJ_TILE_GROUPS):
                 g = i * PROJ_TILE_GROUPS + gi
                 x_pass(
                     h_acc, g, proj_tile[:, gi, :], plane_of_group(proj_planes, g, slice(0, PROJ_N))
                 )
 
-        tail_tile = keep.tile([P, TAIL_N], U32, align_bytes=64)
-        nc.sync.dma_start(out=tail_tile[:].bitcast(I32), in_=tail_words[:, 0, :])
         for r in range(4):
             nc.sync.dma_start(
                 out=tail_planes[r:P:32, 0, :].bitcast(I32),
                 in_=tail_w_0_scales[0, r:SCALE_ROWS:4, :].bitcast(I32),
             )
-        load_scale_planes(nc, head_planes, head_weight_scales)
+        tail_tile = keep.tile([P, TAIL_N], U32, align_bytes=64)
+        nc.sync.dma_start(out=tail_tile[:].bitcast(I32), in_=tail_words[:, 0, :])
+        for q in UPPER_ROWS:
+            load_scale_row(nc, head_planes, head_weight_scales, q)
 
         h_sorted = small.tile([P, PACK, P], BF16)
         nc.scalar.copy(out=h_sorted[:], in_=h_acc[:].rearrange("r (p t) -> r t p", t=PACK))

@@ -14,6 +14,7 @@ COPY = mybir.ActivationFunctionType.Copy
 ADD = mybir.AluOpType.add
 MULT = mybir.AluOpType.mult
 MAX = mybir.AluOpType.max
+MIN = mybir.AluOpType.min
 X_AXIS = mybir.AxisListType.X
 
 P = 128
@@ -27,6 +28,8 @@ HEAD_TOKENS = 1022
 PROJ_N = 512
 TAIL_N = 1024
 HALVES = 2
+HEAD_PIECES = (slice(0, 512), slice(512, 768), slice(768, 1024))
+EARLY_PIECES = 2
 SCALE_ROWS = K_PASS // 32
 PLANE_OFFSETS = 4
 PLANE_SLOTS = GROUPS // PLANE_OFFSETS
@@ -40,9 +43,15 @@ HEAD_TILE_GROUPS = 2
 UPPER_ROWS = range(8, SCALE_ROWS)
 PROJ_ROWS_AFTER_X = ((), range(0, 4), range(4, 8), UPPER_ROWS)
 HEAD_ROWS_AFTER_PROJ = ((), (0, 1), (2, 3), (4, 5), (6, 7), (), (), ())
-HEAD_SPLIT_GROUPS = 4
-TAIL_ON_SCALAR = 688
-HEAD_LAST_LOADS = (2, 1, 1)
+HEAD_LAST_LOADS = (
+    (26, 2, (0, 1)),
+    (28, 2, (0, 1)),
+    (30, 2, (0, 1)),
+    (26, 2, (2,)),
+    (28, 2, (2,)),
+    (30, 2, (2,)),
+)
+TAIL_ON_SCALAR = 640
 
 FLOPS = 2 * P * D * (HEAD_N + PROJ_N) + 2 * P * PROJ_N * TAIL_N
 
@@ -191,7 +200,7 @@ def tile_adaptiveinputsoftmax_pa_k_kernel(
                 stop=(g == GROUPS - 1),
             )
 
-        h_acc = psum.tile([P, PROJ_N], F32)
+        h_acc = psum.tile([P, PROJ_N], F32, tag="h_acc")
         for i in range(GROUPS // PROJ_TILE_GROUPS):
             proj_tile = proj_pool.tile([P, PROJ_TILE_GROUPS, PROJ_N], U32, align_bytes=64)
             nc.sync.dma_start(
@@ -246,117 +255,149 @@ def tile_adaptiveinputsoftmax_pa_k_kernel(
             tail_logits.append(logits)
         tail_exp = keep.tile([P, TAIL_N], F32)
         tail_recip = exp_and_reciprocal(nc, small, tail_logits, tail_exp, "tail")
+        nc.vector.tensor_scalar_mul(out=tail_exp[:], in0=tail_exp[:], scalar1=tail_recip[:])
 
         head_logits = []
-        for b in range(HALVES):
-            logits = psum.tile([P, BANK], F32, name="head_logits%d" % b)
-            head_logits.append(logits)
-        half_columns = [slice(b * BANK, (b + 1) * BANK) for b in range(HALVES)]
-        split_from = GROUPS - HEAD_SPLIT_GROUPS
-        for i in range(split_from // HEAD_TILE_GROUPS):
-            head_tile = head_pool.tile([P, HEAD_TILE_GROUPS, HEAD_N], U32, align_bytes=64)
-            nc.sync.dma_start(
-                out=head_tile[:].bitcast(I32),
-                in_=head_words[:, i * HEAD_TILE_GROUPS : (i + 1) * HEAD_TILE_GROUPS, :],
+        for i, columns in enumerate(HEAD_PIECES):
+            logits = psum.tile(
+                [P, columns.stop - columns.start],
+                F32,
+                tag="h_acc" if i == 1 else "head_logits%d" % i,
+                name="head_logits%d" % i,
             )
-            for b in range(HALVES):
-                for gi in range(HEAD_TILE_GROUPS):
-                    g = i * HEAD_TILE_GROUPS + gi
+            head_logits.append(logits)
+
+        def head_passes(tile, tile_start, g0, count, pieces):
+            for i in pieces:
+                columns = HEAD_PIECES[i]
+                for gi in range(count):
                     x_pass(
-                        head_logits[b],
-                        g,
-                        head_tile[:, gi, half_columns[b]],
-                        plane_of_group(head_planes, g, half_columns[b]),
+                        head_logits[i],
+                        g0 + gi,
+                        tile[:, gi, columns.start - tile_start : columns.stop - tile_start],
+                        plane_of_group(head_planes, g0 + gi, columns),
                     )
-        for b, loads in enumerate(((HEAD_SPLIT_GROUPS,), HEAD_LAST_LOADS)):
-            half_tile = head_pool.tile([P, HEAD_SPLIT_GROUPS, BANK], U32, align_bytes=64, tag="head_tile")
-            first = 0
-            for count in loads:
-                nc.sync.dma_start(
-                    out=half_tile[:, first : first + count, :].bitcast(I32),
-                    in_=head_words[:, split_from + first : split_from + first + count, half_columns[b]],
-                )
-                first += count
-            for gi in range(HEAD_SPLIT_GROUPS):
-                g = split_from + gi
-                x_pass(
-                    head_logits[b],
-                    g,
-                    half_tile[:, gi, :],
-                    plane_of_group(head_planes, g, half_columns[b]),
-                )
+
+        for i in range(HEAD_LAST_LOADS[0][0] // HEAD_TILE_GROUPS):
+            head_tile = head_pool.tile([P, HEAD_TILE_GROUPS, HEAD_N], U32, align_bytes=64)
+            g0 = i * HEAD_TILE_GROUPS
+            nc.sync.dma_start(
+                out=head_tile[:].bitcast(I32), in_=head_words[:, g0 : g0 + HEAD_TILE_GROUPS, :]
+            )
+            head_passes(head_tile, 0, g0, HEAD_TILE_GROUPS, range(len(HEAD_PIECES)))
+        for g0, count, pieces in HEAD_LAST_LOADS:
+            start = HEAD_PIECES[pieces[0]].start
+            stop = HEAD_PIECES[pieces[-1]].stop
+            piece_tile = head_pool.tile(
+                [P, count, stop - start], U32, align_bytes=64, tag="head_tile"
+            )
+            nc.sync.dma_start(
+                out=piece_tile[:].bitcast(I32), in_=head_words[:, g0 : g0 + count, start:stop]
+            )
+            head_passes(piece_tile, start, g0, count, pieces)
 
         head_exp = keep.tile([P, HEAD_N], F32)
-        max0 = small.tile([P, 1], F32)
-        nc.vector.reduce_max(out=max0[:], in_=head_logits[0][:], axis=X_AXIS)
-        neg_max0 = small.tile([P, 1], F32)
-        nc.vector.tensor_scalar_mul(out=neg_max0[:], in0=max0[:], scalar1=-1.0)
-        sum0 = small.tile([P, 1], F32)
-        nc.scalar.activation(
-            out=head_exp[:, half_columns[0]],
-            in_=head_logits[0][:],
-            func=EXP,
-            bias=neg_max0[:],
-            scale=1.0,
-            accum_out=sum0[:],
-        )
-        max1 = small.tile([P, 1], F32)
-        nc.vector.reduce_max(out=max1[:], in_=head_logits[1][:], axis=X_AXIS)
-        neg_max = small.tile([P, 1], F32)
+        piece_max = small.tile([P, len(HEAD_PIECES)], F32)
+        piece_sum = small.tile([P, len(HEAD_PIECES)], F32)
+        neg_early_max = small.tile([P, 1], F32)
+        neg_head_max = small.tile([P, 1], F32)
+
+        def piece_reduce_max(i):
+            nc.vector.reduce_max(
+                out=piece_max[:, i : i + 1], in_=head_logits[i][:], axis=X_AXIS
+            )
+
+        def piece_exp(i, neg_max):
+            nc.scalar.activation(
+                out=head_exp[:, HEAD_PIECES[i]],
+                in_=head_logits[i][:],
+                func=EXP,
+                bias=neg_max[:],
+                scale=1.0,
+                accum_out=piece_sum[:, i : i + 1],
+            )
+
+        for i in range(EARLY_PIECES):
+            piece_reduce_max(i)
         nc.vector.tensor_scalar(
-            out=neg_max[:], in0=max1[:], scalar1=max0[:], scalar2=-1.0, op0=MAX, op1=MULT
+            out=neg_early_max[:],
+            in0=piece_max[:, 0:1],
+            scalar1=piece_max[:, 1:2],
+            scalar2=-1.0,
+            op0=MAX,
+            op1=MULT,
         )
-        shift0 = small.tile([P, 1], F32)
-        nc.scalar.activation(out=shift0[:], in_=max0[:], func=EXP, bias=neg_max[:], scale=1.0)
-        sum1 = small.tile([P, 1], F32)
+        for i in range(EARLY_PIECES):
+            piece_exp(i, neg_early_max)
+        early_sum = small.tile([P, 1], F32)
+        nc.vector.tensor_add(out=early_sum[:], in0=piece_sum[:, 0:1], in1=piece_sum[:, 1:2])
+        piece_reduce_max(EARLY_PIECES)
+        nc.vector.tensor_scalar(
+            out=neg_head_max[:],
+            in0=piece_max[:, 2:3],
+            scalar1=-1.0,
+            scalar2=neg_early_max[:],
+            op0=MULT,
+            op1=MIN,
+        )
+        shift = small.tile([P, 1], F32)
         nc.scalar.activation(
-            out=head_exp[:, half_columns[1]],
-            in_=head_logits[1][:],
-            func=EXP,
-            bias=neg_max[:],
-            scale=1.0,
-            accum_out=sum1[:],
+            out=shift[:], in_=neg_early_max[:], func=EXP, bias=neg_head_max[:], scale=-1.0
         )
+        piece_exp(EARLY_PIECES, neg_head_max)
         total = small.tile([P, 1], F32)
         nc.vector.scalar_tensor_tensor(
-            out=total[:], in0=sum0[:], scalar=shift0[:], in1=sum1[:], op0=MULT, op1=ADD
+            out=total[:],
+            in0=early_sum[:],
+            scalar=shift[:],
+            in1=piece_sum[:, 2:3],
+            op0=MULT,
+            op1=ADD,
         )
         recip = small.tile([P, 1], F32)
         nc.vector.reciprocal(out=recip[:], in_=total[:])
 
-        tail_factor = small.tile([P, 1], F32)
-        nc.vector.tensor_scalar(
-            out=tail_factor[:],
-            in0=head_exp[:, HEAD_TOKENS : HEAD_TOKENS + 1],
-            scalar1=recip[:],
-            scalar2=tail_recip[:],
-            op0=MULT,
-            op1=MULT,
+        nc.scalar.activation(
+            out=tail_exp[:],
+            in_=tail_exp[:],
+            func=COPY,
+            scale=head_exp[:, HEAD_TOKENS : HEAD_TOKENS + 1],
         )
         nc.scalar.activation(
             out=tail_exp[:, 0:TAIL_ON_SCALAR],
             in_=tail_exp[:, 0:TAIL_ON_SCALAR],
             func=COPY,
-            scale=tail_factor[:],
+            scale=recip[:],
         )
+        nc.vector.tensor_scalar(
+            out=head_exp[:, HEAD_PIECES[0]],
+            in0=head_exp[:, HEAD_PIECES[0]],
+            scalar1=recip[:],
+            scalar2=shift[:],
+            op0=MULT,
+            op1=MULT,
+        )
+        nc.sync.dma_start(out=probs_rows[:, HEAD_PIECES[0]], in_=head_exp[:, HEAD_PIECES[0]])
         other = small.tile([P, 1], F32)
         nc.vector.tensor_scalar_mul(
             out=other[:], in0=head_exp[:, HEAD_N - 1 : HEAD_N], scalar1=recip[:]
         )
-        nc.vector.tensor_scalar_mul(
-            out=head_exp[:, BANK:HEAD_TOKENS], in0=head_exp[:, BANK:HEAD_TOKENS], scalar1=recip[:]
-        )
         nc.vector.tensor_scalar(
-            out=head_exp[:, 0:BANK],
-            in0=head_exp[:, 0:BANK],
+            out=head_exp[:, HEAD_PIECES[1]],
+            in0=head_exp[:, HEAD_PIECES[1]],
             scalar1=recip[:],
-            scalar2=shift0[:],
+            scalar2=shift[:],
             op0=MULT,
             op1=MULT,
         )
-        nc.sync.dma_start(out=probs_rows[:, 0:HEAD_TOKENS], in_=head_exp[:, 0:HEAD_TOKENS])
+        last_piece = slice(HEAD_PIECES[2].start, HEAD_TOKENS)
         nc.vector.tensor_scalar_mul(
-            out=tail_exp[:, TAIL_ON_SCALAR:], in0=tail_exp[:, TAIL_ON_SCALAR:], scalar1=tail_factor[:]
+            out=head_exp[:, last_piece], in0=head_exp[:, last_piece], scalar1=recip[:]
+        )
+        later_pieces = slice(HEAD_PIECES[1].start, HEAD_TOKENS)
+        nc.sync.dma_start(out=probs_rows[:, later_pieces], in_=head_exp[:, later_pieces])
+        nc.vector.tensor_scalar_mul(
+            out=tail_exp[:, TAIL_ON_SCALAR:], in0=tail_exp[:, TAIL_ON_SCALAR:], scalar1=recip[:]
         )
         nc.sync.dma_start(out=probs_rows[:, HEAD_TOKENS : HEAD_TOKENS + TAIL_N], in_=tail_exp[:])
 

@@ -40,18 +40,34 @@ BANK_GROUPS = 2
 PROJ_TILE_GROUPS = 4
 HEAD_TILE_GROUPS = 2
 
-UPPER_ROWS = range(8, SCALE_ROWS)
-PROJ_ROWS_AFTER_X = ((), range(0, 4), range(4, 8), UPPER_ROWS)
-HEAD_ROWS_AFTER_PROJ = ((), (0, 1), (2, 3), (4, 5), (6, 7), (), (), ())
+PROJ, HEAD = 0, 1
+SCALE_ROWS_AFTER_X = (
+    (),
+    tuple((PROJ, q) for q in range(0, 4)),
+    tuple((PROJ, q) for q in range(4, 8)),
+    tuple((weight, q) for q in range(8, SCALE_ROWS) for weight in (HEAD, PROJ)),
+)
+SCALE_ROWS_AFTER_PROJ = (
+    ((HEAD, 0), (HEAD, 1)),
+    ((HEAD, 2), (HEAD, 3)),
+    ((HEAD, 4), (HEAD, 5)),
+    ((HEAD, 6), (HEAD, 7)),
+    (),
+    (),
+    (),
+    (),
+)
 HEAD_LAST_LOADS = (
     (26, 2, (0, 1)),
     (28, 2, (0, 1)),
     (30, 2, (0, 1)),
     (26, 2, (2,)),
     (28, 2, (2,)),
-    (30, 2, (2,)),
+    (30, 1, (2,)),
+    (31, 1, (2,)),
 )
-TAIL_ON_SCALAR = 640
+FIRST_STORE = slice(0, 256)
+TAIL_ON_SCALAR = 512
 
 FLOPS = 2 * P * D * (HEAD_N + PROJ_N) + 2 * P * PROJ_N * TAIL_N
 
@@ -144,6 +160,11 @@ def tile_adaptiveinputsoftmax_pa_k_kernel(
         for planes in (proj_planes, tail_planes, head_planes):
             nc.vector.memset(planes[:].bitcast(I32), 0)
 
+        scale_planes = {
+            PROJ: (proj_planes, tail_proj_0_scales),
+            HEAD: (head_planes, head_weight_scales),
+        }
+
         chunk_columns = X_CHUNK_GROUPS * K_PASS
         x_chunks = []
         for c in range(GROUPS // X_CHUNK_GROUPS):
@@ -152,8 +173,8 @@ def tile_adaptiveinputsoftmax_pa_k_kernel(
                 out=x_chunk[:], in_=x_rows[:, c * chunk_columns : (c + 1) * chunk_columns]
             )
             x_chunks.append(x_chunk)
-            for q in PROJ_ROWS_AFTER_X[c]:
-                load_scale_row(nc, proj_planes, tail_proj_0_scales, q)
+            for weight, q in SCALE_ROWS_AFTER_X[c]:
+                load_scale_row(nc, *scale_planes[weight], q)
 
         x_codes = keep.tile([P, GROUPS * P], U32, align_bytes=64)
         x_scales = keep.tile([P, GROUPS * P], U8, align_bytes=64)
@@ -207,8 +228,8 @@ def tile_adaptiveinputsoftmax_pa_k_kernel(
                 out=proj_tile[:].bitcast(I32),
                 in_=proj_words[:, i * PROJ_TILE_GROUPS : (i + 1) * PROJ_TILE_GROUPS, :],
             )
-            for q in HEAD_ROWS_AFTER_PROJ[i]:
-                load_scale_row(nc, head_planes, head_weight_scales, q)
+            for weight, q in SCALE_ROWS_AFTER_PROJ[i]:
+                load_scale_row(nc, *scale_planes[weight], q)
             for gi in range(PROJ_TILE_GROUPS):
                 g = i * PROJ_TILE_GROUPS + gi
                 x_pass(
@@ -222,8 +243,6 @@ def tile_adaptiveinputsoftmax_pa_k_kernel(
             )
         tail_tile = keep.tile([P, TAIL_N], U32, align_bytes=64)
         nc.sync.dma_start(out=tail_tile[:].bitcast(I32), in_=tail_words[:, 0, :])
-        for q in UPPER_ROWS:
-            load_scale_row(nc, head_planes, head_weight_scales, q)
 
         h_sorted = small.tile([P, PACK, P], BF16)
         nc.scalar.copy(out=h_sorted[:], in_=h_acc[:].rearrange("r (p t) -> r t p", t=PACK))
@@ -357,11 +376,12 @@ def tile_adaptiveinputsoftmax_pa_k_kernel(
         recip = small.tile([P, 1], F32)
         nc.vector.reciprocal(out=recip[:], in_=total[:])
 
+        cluster_exp = head_exp[:, HEAD_TOKENS : HEAD_TOKENS + 1]
         nc.scalar.activation(
-            out=tail_exp[:],
-            in_=tail_exp[:],
+            out=tail_exp[:, 0:TAIL_ON_SCALAR],
+            in_=tail_exp[:, 0:TAIL_ON_SCALAR],
             func=COPY,
-            scale=head_exp[:, HEAD_TOKENS : HEAD_TOKENS + 1],
+            scale=cluster_exp,
         )
         nc.scalar.activation(
             out=tail_exp[:, 0:TAIL_ON_SCALAR],
@@ -369,35 +389,37 @@ def tile_adaptiveinputsoftmax_pa_k_kernel(
             func=COPY,
             scale=recip[:],
         )
-        nc.vector.tensor_scalar(
-            out=head_exp[:, HEAD_PIECES[0]],
-            in0=head_exp[:, HEAD_PIECES[0]],
-            scalar1=recip[:],
-            scalar2=shift[:],
-            op0=MULT,
-            op1=MULT,
-        )
-        nc.sync.dma_start(out=probs_rows[:, HEAD_PIECES[0]], in_=head_exp[:, HEAD_PIECES[0]])
+
+        def scale_early_head(columns):
+            nc.vector.tensor_scalar(
+                out=head_exp[:, columns],
+                in0=head_exp[:, columns],
+                scalar1=recip[:],
+                scalar2=shift[:],
+                op0=MULT,
+                op1=MULT,
+            )
+
+        scale_early_head(FIRST_STORE)
+        nc.sync.dma_start(out=probs_rows[:, FIRST_STORE], in_=head_exp[:, FIRST_STORE])
         other = small.tile([P, 1], F32)
         nc.vector.tensor_scalar_mul(
             out=other[:], in0=head_exp[:, HEAD_N - 1 : HEAD_N], scalar1=recip[:]
         )
-        nc.vector.tensor_scalar(
-            out=head_exp[:, HEAD_PIECES[1]],
-            in0=head_exp[:, HEAD_PIECES[1]],
-            scalar1=recip[:],
-            scalar2=shift[:],
-            op0=MULT,
-            op1=MULT,
-        )
+        scale_early_head(slice(FIRST_STORE.stop, HEAD_PIECES[EARLY_PIECES].start))
         last_piece = slice(HEAD_PIECES[2].start, HEAD_TOKENS)
         nc.vector.tensor_scalar_mul(
             out=head_exp[:, last_piece], in0=head_exp[:, last_piece], scalar1=recip[:]
         )
-        later_pieces = slice(HEAD_PIECES[1].start, HEAD_TOKENS)
+        later_pieces = slice(FIRST_STORE.stop, HEAD_TOKENS)
         nc.sync.dma_start(out=probs_rows[:, later_pieces], in_=head_exp[:, later_pieces])
-        nc.vector.tensor_scalar_mul(
-            out=tail_exp[:, TAIL_ON_SCALAR:], in0=tail_exp[:, TAIL_ON_SCALAR:], scalar1=recip[:]
+        nc.vector.tensor_scalar(
+            out=tail_exp[:, TAIL_ON_SCALAR:],
+            in0=tail_exp[:, TAIL_ON_SCALAR:],
+            scalar1=cluster_exp,
+            scalar2=recip[:],
+            op0=MULT,
+            op1=MULT,
         )
         nc.sync.dma_start(out=probs_rows[:, HEAD_TOKENS : HEAD_TOKENS + TAIL_N], in_=tail_exp[:])
 

@@ -66,7 +66,6 @@ HEAD_LAST_LOADS = (
     (30, 1, (2,)),
     (31, 1, (2,)),
 )
-FIRST_STORE = slice(0, 256)
 TAIL_ON_SCALAR = 512
 
 FLOPS = 2 * P * D * (HEAD_N + PROJ_N) + 2 * P * PROJ_N * TAIL_N
@@ -377,6 +376,7 @@ def tile_adaptiveinputsoftmax_pa_k_kernel(
         nc.vector.reciprocal(out=recip[:], in_=total[:])
 
         cluster_exp = head_exp[:, HEAD_TOKENS : HEAD_TOKENS + 1]
+        out_rows = keep.tile([P, HEAD_TOKENS + TAIL_N], F32)
         nc.scalar.activation(
             out=tail_exp[:, 0:TAIL_ON_SCALAR],
             in_=tail_exp[:, 0:TAIL_ON_SCALAR],
@@ -384,44 +384,37 @@ def tile_adaptiveinputsoftmax_pa_k_kernel(
             scale=cluster_exp,
         )
         nc.scalar.activation(
-            out=tail_exp[:, 0:TAIL_ON_SCALAR],
+            out=out_rows[:, HEAD_TOKENS : HEAD_TOKENS + TAIL_ON_SCALAR],
             in_=tail_exp[:, 0:TAIL_ON_SCALAR],
             func=COPY,
             scale=recip[:],
         )
-
-        def scale_early_head(columns):
-            nc.vector.tensor_scalar(
-                out=head_exp[:, columns],
-                in0=head_exp[:, columns],
-                scalar1=recip[:],
-                scalar2=shift[:],
-                op0=MULT,
-                op1=MULT,
-            )
-
-        scale_early_head(FIRST_STORE)
-        nc.sync.dma_start(out=probs_rows[:, FIRST_STORE], in_=head_exp[:, FIRST_STORE])
+        early_columns = slice(0, HEAD_PIECES[EARLY_PIECES].start)
+        nc.vector.tensor_scalar(
+            out=out_rows[:, early_columns],
+            in0=head_exp[:, early_columns],
+            scalar1=recip[:],
+            scalar2=shift[:],
+            op0=MULT,
+            op1=MULT,
+        )
         other = small.tile([P, 1], F32)
         nc.vector.tensor_scalar_mul(
             out=other[:], in0=head_exp[:, HEAD_N - 1 : HEAD_N], scalar1=recip[:]
         )
-        scale_early_head(slice(FIRST_STORE.stop, HEAD_PIECES[EARLY_PIECES].start))
-        last_piece = slice(HEAD_PIECES[2].start, HEAD_TOKENS)
+        last_piece = slice(HEAD_PIECES[EARLY_PIECES].start, HEAD_TOKENS)
         nc.vector.tensor_scalar_mul(
-            out=head_exp[:, last_piece], in0=head_exp[:, last_piece], scalar1=recip[:]
+            out=out_rows[:, last_piece], in0=head_exp[:, last_piece], scalar1=recip[:]
         )
-        later_pieces = slice(FIRST_STORE.stop, HEAD_TOKENS)
-        nc.sync.dma_start(out=probs_rows[:, later_pieces], in_=head_exp[:, later_pieces])
         nc.vector.tensor_scalar(
-            out=tail_exp[:, TAIL_ON_SCALAR:],
+            out=out_rows[:, HEAD_TOKENS + TAIL_ON_SCALAR :],
             in0=tail_exp[:, TAIL_ON_SCALAR:],
             scalar1=cluster_exp,
             scalar2=recip[:],
             op0=MULT,
             op1=MULT,
         )
-        nc.sync.dma_start(out=probs_rows[:, HEAD_TOKENS : HEAD_TOKENS + TAIL_N], in_=tail_exp[:])
+        nc.sync.dma_start(out=probs_rows, in_=out_rows[:])
 
         other_t = psum.tile([P, P], F32, tag="transposed", bufs=3)
         nc.tensor.matmul(

@@ -45,13 +45,14 @@ SCALE_ROWS_AFTER_X = (
     (),
     tuple((PROJ, q) for q in range(0, 4)),
     tuple((PROJ, q) for q in range(4, 8)),
-    tuple((weight, q) for q in range(8, SCALE_ROWS) for weight in (HEAD, PROJ)),
+    tuple((weight, q) for q in range(8, SCALE_ROWS) for weight in (HEAD, PROJ))
+    + ((HEAD, 0), (HEAD, 1)),
 )
 SCALE_ROWS_AFTER_PROJ = (
-    ((HEAD, 0), (HEAD, 1)),
     ((HEAD, 2), (HEAD, 3)),
     ((HEAD, 4), (HEAD, 5)),
     ((HEAD, 6), (HEAD, 7)),
+    (),
     (),
     (),
     (),

from contextlib import ExitStack

import concourse.mybir as mybir
from concourse.masks import make_identity

F32 = mybir.dt.float32
BF16 = mybir.dt.bfloat16
I32 = mybir.dt.int32
U32 = mybir.dt.uint32
U8 = mybir.dt.uint8
FP8X4 = mybir.dt.float8_e4m3fn_x4
EXP = mybir.ActivationFunctionType.Exp
COPY = mybir.ActivationFunctionType.Copy
ADD = mybir.AluOpType.add
MULT = mybir.AluOpType.mult
MAX = mybir.AluOpType.max
MIN = mybir.AluOpType.min
X_AXIS = mybir.AxisListType.X

P = 128
PACK = 4
K_PASS = P * PACK
D = 16384
GROUPS = D // K_PASS
BANK = 512
HEAD_N = 1024
HEAD_TOKENS = 1022
PROJ_N = 512
TAIL_N = 1024
HALVES = 2
HEAD_PIECES = (slice(0, 512), slice(512, 768), slice(768, 1024))
EARLY_PIECES = 2
SCALE_ROWS = K_PASS // 32
PLANE_OFFSETS = 4
PLANE_SLOTS = GROUPS // PLANE_OFFSETS

X_CHUNK_GROUPS = 8
QUANT_GROUPS = 4
BANK_GROUPS = 2
PROJ_TILE_GROUPS = 4
HEAD_TILE_GROUPS = 2

PROJ, HEAD = 0, 1
SCALE_ROWS_AFTER_X = (
    (),
    tuple((PROJ, q) for q in range(0, 4)),
    tuple((PROJ, q) for q in range(4, 8)),
    tuple((weight, q) for q in range(8, SCALE_ROWS) for weight in (HEAD, PROJ))
    + ((HEAD, 0), (HEAD, 1)),
)
SCALE_ROWS_AFTER_PROJ = (
    ((HEAD, 2), (HEAD, 3)),
    ((HEAD, 4), (HEAD, 5)),
    ((HEAD, 6), (HEAD, 7)),
    (),
    (),
    (),
    (),
    (),
)
HEAD_LAST_LOADS = (
    (26, 2, (0, 1)),
    (28, 2, (0, 1)),
    (30, 2, (0, 1)),
    (26, 2, (2,)),
    (28, 2, (2,)),
    (30, 1, (2,)),
    (31, 1, (2,)),
)
TAIL_ON_SCALAR = 512

FLOPS = 2 * P * D * (HEAD_N + PROJ_N) + 2 * P * PROJ_N * TAIL_N


def words_by_partition(words):
    return words.rearrange("g p n t -> p g (n t)").bitcast(I32)


def load_scale_row(nc, planes, scales, q):
    slots = planes.shape[1]
    first = 32 * (q // 4) + q % 4
    nc.sync.dma_start(
        out=planes[first : first + 4 * PLANE_OFFSETS : 4].bitcast(I32),
        in_=scales[:, q, :].rearrange("(j a) n -> j a n", a=slots).bitcast(I32),
    )


def plane_of_group(planes, g, columns):
    slots = planes.shape[1]
    return planes[4 * (g // slots) : P, g % slots, columns]


def exp_and_reciprocal(nc, small, logits, exps, label):
    bank_max = small.tile([P, HALVES], F32, name=label + "_bank_max")
    for b in range(HALVES):
        nc.vector.reduce_max(out=bank_max[:, b : b + 1], in_=logits[b][:], axis=X_AXIS)
    neg_max = small.tile([P, 1], F32, name=label + "_neg_max")
    nc.vector.tensor_scalar(
        out=neg_max[:],
        in0=bank_max[:, 0:1],
        scalar1=bank_max[:, 1:2],
        scalar2=-1.0,
        op0=MAX,
        op1=MULT,
    )
    bank_sum = small.tile([P, HALVES], F32, name=label + "_bank_sum")
    for b in range(HALVES):
        nc.scalar.activation(
            out=exps[:, b * BANK : (b + 1) * BANK],
            in_=logits[b][:],
            func=EXP,
            bias=neg_max[:],
            scale=1.0,
            accum_out=bank_sum[:, b : b + 1],
        )
    total = small.tile([P, 1], F32, name=label + "_total")
    nc.vector.tensor_add(out=total[:], in0=bank_sum[:, 0:1], in1=bank_sum[:, 1:2])
    recip = small.tile([P, 1], F32, name=label + "_recip")
    nc.vector.reciprocal(out=recip[:], in_=total[:])
    return recip


def tile_adaptiveinputsoftmax_pa_k_kernel(
    tc,
    x,
    head_weight_words,
    head_weight_scales,
    tail_proj_0_words,
    tail_proj_0_scales,
    tail_w_0_words,
    tail_w_0_scales,
    out_0,
    out_1,
):
    nc = tc.nc
    x_rows = x.flatten_outer_dims()
    probs_rows = out_0.flatten_outer_dims()
    other_row = out_1.rearrange("a b c -> c (a b)")
    head_words = words_by_partition(head_weight_words)
    proj_words = words_by_partition(tail_proj_0_words)
    tail_words = words_by_partition(tail_w_0_words)

    with ExitStack() as stack:
        keep = stack.enter_context(tc.tile_pool(name="keep", bufs=1))
        small = stack.enter_context(tc.tile_pool(name="small", bufs=1))
        x_pool = stack.enter_context(tc.tile_pool(name="x_pool", bufs=4))
        stage = stack.enter_context(tc.tile_pool(name="stage", bufs=3))
        proj_pool = stack.enter_context(tc.tile_pool(name="proj_pool", bufs=8))
        head_pool = stack.enter_context(tc.tile_pool(name="head_pool", bufs=6))
        psum = stack.enter_context(tc.psum_pool(name="psum", bufs=1))

        ident_f32 = keep.tile([P, P], F32)
        make_identity(nc, ident_f32[:])
        ident_bf16 = keep.tile([P, P], BF16)
        make_identity(nc, ident_bf16[:])

        proj_planes = keep.tile([P, PLANE_SLOTS, PROJ_N], U8, align_bytes=64)
        tail_planes = keep.tile([P, 1, TAIL_N], U8, align_bytes=64)
        head_planes = keep.tile([P, PLANE_SLOTS, HEAD_N], U8, align_bytes=64)
        for planes in (proj_planes, tail_planes, head_planes):
            nc.vector.memset(planes[:].bitcast(I32), 0)

        scale_planes = {
            PROJ: (proj_planes, tail_proj_0_scales),
            HEAD: (head_planes, head_weight_scales),
        }

        chunk_columns = X_CHUNK_GROUPS * K_PASS
        x_chunks = []
        for c in range(GROUPS // X_CHUNK_GROUPS):
            x_chunk = x_pool.tile([P, chunk_columns], BF16)
            nc.sync.dma_start(
                out=x_chunk[:], in_=x_rows[:, c * chunk_columns : (c + 1) * chunk_columns]
            )
            x_chunks.append(x_chunk)
            for weight, q in SCALE_ROWS_AFTER_X[c]:
                load_scale_row(nc, *scale_planes[weight], q)

        x_codes = keep.tile([P, GROUPS * P], U32, align_bytes=64)
        x_scales = keep.tile([P, GROUPS * P], U8, align_bytes=64)
        for c in range(GROUPS // X_CHUNK_GROUPS):
            x_chunk = x_chunks[c]
            x_pairs = x_chunk[:].bitcast(F32)
            for call in range(X_CHUNK_GROUPS // QUANT_GROUPS):
                grouped = stage.tile([P, QUANT_GROUPS * K_PASS], BF16, align_bytes=64)
                grouped_pairs = grouped[:].bitcast(F32)
                for bank in range(QUANT_GROUPS // BANK_GROUPS):
                    xt = psum.tile([P, BANK_GROUPS, 2, P], F32, tag="transposed", bufs=3)
                    for gi in range(BANK_GROUPS):
                        first = (K_PASS // 2) * (call * QUANT_GROUPS + bank * BANK_GROUPS + gi)
                        for u in range(2):
                            nc.tensor.transpose(
                                xt[:, gi, u, :],
                                x_pairs[:, first + u : first + K_PASS // 2 : 2],
                                ident_f32[:],
                            )
                    pairs_out = grouped_pairs[:, bank * BANK : (bank + 1) * BANK].rearrange(
                        "p (g r u) -> p g r u", g=BANK_GROUPS, u=2
                    )
                    pairs_in = xt[:].rearrange("p g u r -> p g r u")
                    if bank % 2 == 0:
                        nc.scalar.copy(out=pairs_out, in_=pairs_in)
                    else:
                        nc.vector.tensor_copy(out=pairs_out, in_=pairs_in)
                g0 = c * X_CHUNK_GROUPS + call * QUANT_GROUPS
                columns = slice(g0 * P, (g0 + QUANT_GROUPS) * P)
                nc.vector.quantize_mx(
                    out=x_codes[:, columns].bitcast(FP8X4),
                    scales=x_scales[:, columns],
                    in_=grouped[:],
                )

        def x_pass(acc, g, weight_words, weight_plane):
            nc.tensor.matmul_mx(
                out=acc[:],
                lhsT=x_codes[:, g * P : (g + 1) * P].bitcast(FP8X4),
                lhsT_scale=x_scales[:, g * P : (g + 1) * P],
                rhs=weight_words.bitcast(FP8X4),
                rhs_scale=weight_plane,
                start=(g == 0),
                stop=(g == GROUPS - 1),
            )

        h_acc = psum.tile([P, PROJ_N], F32, tag="h_acc")
        for i in range(GROUPS // PROJ_TILE_GROUPS):
            proj_tile = proj_pool.tile([P, PROJ_TILE_GROUPS, PROJ_N], U32, align_bytes=64)
            nc.sync.dma_start(
                out=proj_tile[:].bitcast(I32),
                in_=proj_words[:, i * PROJ_TILE_GROUPS : (i + 1) * PROJ_TILE_GROUPS, :],
            )
            for weight, q in SCALE_ROWS_AFTER_PROJ[i]:
                load_scale_row(nc, *scale_planes[weight], q)
            for gi in range(PROJ_TILE_GROUPS):
                g = i * PROJ_TILE_GROUPS + gi
                x_pass(
                    h_acc, g, proj_tile[:, gi, :], plane_of_group(proj_planes, g, slice(0, PROJ_N))
                )

        for r in range(4):
            nc.sync.dma_start(
                out=tail_planes[r:P:32, 0, :].bitcast(I32),
                in_=tail_w_0_scales[0, r:SCALE_ROWS:4, :].bitcast(I32),
            )
        tail_tile = keep.tile([P, TAIL_N], U32, align_bytes=64)
        nc.sync.dma_start(out=tail_tile[:].bitcast(I32), in_=tail_words[:, 0, :])

        h_sorted = small.tile([P, PACK, P], BF16)
        nc.scalar.copy(out=h_sorted[:], in_=h_acc[:].rearrange("r (p t) -> r t p", t=PACK))
        ht = psum.tile([P, PACK, P], BF16, tag="transposed", bufs=3)
        for t in range(PACK):
            nc.tensor.transpose(ht[:, t, :], h_sorted[:, t, :], ident_bf16[:])
        h_grouped = small.tile([P, P, PACK], BF16, align_bytes=64)
        nc.vector.tensor_copy(out=h_grouped[:], in_=ht[:].rearrange("p t r -> p r t"))
        h_codes = small.tile([P, P], U32, align_bytes=64)
        h_scales = small.tile([P, P], U8, align_bytes=64)
        nc.vector.quantize_mx(
            out=h_codes[:].bitcast(FP8X4),
            scales=h_scales[:],
            in_=h_grouped[:].rearrange("p r t -> p (r t)"),
        )
        tail_logits = []
        for b in range(HALVES):
            columns = slice(b * BANK, (b + 1) * BANK)
            logits = psum.tile([P, BANK], F32, name="tail_logits%d" % b)
            nc.tensor.matmul_mx(
                out=logits[:],
                lhsT=h_codes[:].bitcast(FP8X4),
                lhsT_scale=h_scales[:],
                rhs=tail_tile[:, columns].bitcast(FP8X4),
                rhs_scale=plane_of_group(tail_planes, 0, columns),
                start=True,
                stop=True,
            )
            tail_logits.append(logits)
        tail_exp = keep.tile([P, TAIL_N], F32)
        tail_recip = exp_and_reciprocal(nc, small, tail_logits, tail_exp, "tail")
        nc.vector.tensor_scalar_mul(out=tail_exp[:], in0=tail_exp[:], scalar1=tail_recip[:])

        head_logits = []
        for i, columns in enumerate(HEAD_PIECES):
            logits = psum.tile(
                [P, columns.stop - columns.start],
                F32,
                tag="h_acc" if i == 1 else "head_logits%d" % i,
                name="head_logits%d" % i,
            )
            head_logits.append(logits)

        def head_passes(tile, tile_start, g0, count, pieces):
            for i in pieces:
                columns = HEAD_PIECES[i]
                for gi in range(count):
                    x_pass(
                        head_logits[i],
                        g0 + gi,
                        tile[:, gi, columns.start - tile_start : columns.stop - tile_start],
                        plane_of_group(head_planes, g0 + gi, columns),
                    )

        for i in range(HEAD_LAST_LOADS[0][0] // HEAD_TILE_GROUPS):
            head_tile = head_pool.tile([P, HEAD_TILE_GROUPS, HEAD_N], U32, align_bytes=64)
            g0 = i * HEAD_TILE_GROUPS
            nc.sync.dma_start(
                out=head_tile[:].bitcast(I32), in_=head_words[:, g0 : g0 + HEAD_TILE_GROUPS, :]
            )
            head_passes(head_tile, 0, g0, HEAD_TILE_GROUPS, range(len(HEAD_PIECES)))
        for g0, count, pieces in HEAD_LAST_LOADS:
            start = HEAD_PIECES[pieces[0]].start
            stop = HEAD_PIECES[pieces[-1]].stop
            piece_tile = head_pool.tile(
                [P, count, stop - start], U32, align_bytes=64, tag="head_tile"
            )
            nc.sync.dma_start(
                out=piece_tile[:].bitcast(I32), in_=head_words[:, g0 : g0 + count, start:stop]
            )
            head_passes(piece_tile, start, g0, count, pieces)

        head_exp = keep.tile([P, HEAD_N], F32)
        piece_max = small.tile([P, len(HEAD_PIECES)], F32)
        piece_sum = small.tile([P, len(HEAD_PIECES)], F32)
        neg_early_max = small.tile([P, 1], F32)
        neg_head_max = small.tile([P, 1], F32)

        def piece_reduce_max(i):
            nc.vector.reduce_max(
                out=piece_max[:, i : i + 1], in_=head_logits[i][:], axis=X_AXIS
            )

        def piece_exp(i, neg_max):
            nc.scalar.activation(
                out=head_exp[:, HEAD_PIECES[i]],
                in_=head_logits[i][:],
                func=EXP,
                bias=neg_max[:],
                scale=1.0,
                accum_out=piece_sum[:, i : i + 1],
            )

        for i in range(EARLY_PIECES):
            piece_reduce_max(i)
        nc.vector.tensor_scalar(
            out=neg_early_max[:],
            in0=piece_max[:, 0:1],
            scalar1=piece_max[:, 1:2],
            scalar2=-1.0,
            op0=MAX,
            op1=MULT,
        )
        for i in range(EARLY_PIECES):
            piece_exp(i, neg_early_max)
        early_sum = small.tile([P, 1], F32)
        nc.vector.tensor_add(out=early_sum[:], in0=piece_sum[:, 0:1], in1=piece_sum[:, 1:2])
        piece_reduce_max(EARLY_PIECES)
        nc.vector.tensor_scalar(
            out=neg_head_max[:],
            in0=piece_max[:, 2:3],
            scalar1=-1.0,
            scalar2=neg_early_max[:],
            op0=MULT,
            op1=MIN,
        )
        shift = small.tile([P, 1], F32)
        nc.scalar.activation(
            out=shift[:], in_=neg_early_max[:], func=EXP, bias=neg_head_max[:], scale=-1.0
        )
        piece_exp(EARLY_PIECES, neg_head_max)
        total = small.tile([P, 1], F32)
        nc.vector.scalar_tensor_tensor(
            out=total[:],
            in0=early_sum[:],
            scalar=shift[:],
            in1=piece_sum[:, 2:3],
            op0=MULT,
            op1=ADD,
        )
        recip = small.tile([P, 1], F32)
        nc.vector.reciprocal(out=recip[:], in_=total[:])

        cluster_exp = head_exp[:, HEAD_TOKENS : HEAD_TOKENS + 1]
        out_rows = keep.tile([P, HEAD_TOKENS + TAIL_N], F32)
        nc.scalar.activation(
            out=tail_exp[:, 0:TAIL_ON_SCALAR],
            in_=tail_exp[:, 0:TAIL_ON_SCALAR],
            func=COPY,
            scale=cluster_exp,
        )
        nc.scalar.activation(
            out=out_rows[:, HEAD_TOKENS : HEAD_TOKENS + TAIL_ON_SCALAR],
            in_=tail_exp[:, 0:TAIL_ON_SCALAR],
            func=COPY,
            scale=recip[:],
        )
        early_columns = slice(0, HEAD_PIECES[EARLY_PIECES].start)
        nc.vector.tensor_scalar(
            out=out_rows[:, early_columns],
            in0=head_exp[:, early_columns],
            scalar1=recip[:],
            scalar2=shift[:],
            op0=MULT,
            op1=MULT,
        )
        other = small.tile([P, 1], F32)
        nc.vector.tensor_scalar_mul(
            out=other[:], in0=head_exp[:, HEAD_N - 1 : HEAD_N], scalar1=recip[:]
        )
        last_piece = slice(HEAD_PIECES[EARLY_PIECES].start, HEAD_TOKENS)
        nc.vector.tensor_scalar_mul(
            out=out_rows[:, last_piece], in0=head_exp[:, last_piece], scalar1=recip[:]
        )
        nc.vector.tensor_scalar(
            out=out_rows[:, HEAD_TOKENS + TAIL_ON_SCALAR :],
            in0=tail_exp[:, TAIL_ON_SCALAR:],
            scalar1=cluster_exp,
            scalar2=recip[:],
            op0=MULT,
            op1=MULT,
        )
        nc.sync.dma_start(out=probs_rows, in_=out_rows[:])

        other_t = psum.tile([P, P], F32, tag="transposed", bufs=3)
        nc.tensor.matmul(
            other_t[:], lhsT=other[:].to_broadcast([P, P]), rhs=ident_f32[:], start=True, stop=True
        )
        other_values = small.tile([1, P], F32)
        nc.vector.tensor_copy(out=other_values[:], in_=other_t[0:1, :])
        nc.sync.dma_start(out=other_row, in_=other_values[:])
